import numpy as np
import ml_dtypes


def mxq(x, axis, fmt="e4m3"):
    dtype, down = {"e4m3": (ml_dtypes.float8_e4m3fn, 7), "e5m2": (ml_dtypes.float8_e5m2, 14)}[fmt]
    v = np.moveaxis(np.asarray(x, np.float32).astype(ml_dtypes.bfloat16).astype(np.float64), axis, -1)
    blocks = v.reshape(v.shape[:-1] + (-1, 32))
    amax = np.abs(blocks).max(-1, keepdims=True)
    byte = np.maximum(np.where(amax > 0, np.frexp(amax)[1] - 1 + 127, 0) - down, 1)
    scale = np.exp2(byte - 127.0)
    codes = (blocks / scale).astype(np.float32).astype(dtype).astype(np.float64)
    return np.moveaxis((codes * scale).reshape(v.shape), -1, axis)


WIDE = False


def mx_kscale(k):
    if not WIDE:
        return np.ones(k)
    levels = np.array([10, -10, 5, -5, 0])
    a = np.random.permutation(np.resize(levels, k // 512 * 4)).reshape(k // 512, 4)
    idx = np.arange(k)
    return np.exp2(a[idx // 512, idx % 128 // 32])


BF16 = ml_dtypes.bfloat16


def bf(x):
    return np.asarray(x, np.float32).astype(BF16)


def f64(x):
    return np.asarray(x).astype(np.float64)


B, D, U1, U2 = 8192, 512, 512, 256
THRESHOLD = 1.0


def setup_inputs():
    s, t = mx_kscale(D), mx_kscale(U1)
    c = s / s.mean()
    u = np.random.random(B)
    target = np.where(np.random.random(B) < 0.5, 0.5 + 0.35 * u, 1.15 + 0.45 * u)
    g = np.random.standard_normal((B, D)) * c
    x = g * (target / np.mean(np.abs(g), axis=1))[:, None]
    return {"x": bf(x),
            "W1": bf(np.random.standard_normal((U1, D)) / np.sqrt(D) / c[None, :] * t[:, None]),
            "b1": bf(np.random.standard_normal(U1) * 0.3 * t),
            "W2": bf(np.random.standard_normal((U2, D)) / np.sqrt(D) / c[None, :] * t[:U2, None]),
            "b2": bf(np.random.standard_normal(U2) * 0.3 * t[:U2]),
            "Wf": bf(np.random.standard_normal((D, U1)) * 1.5 / np.sqrt(U1) / t[None, :]),
            "bf": bf(np.random.standard_normal(D) * 0.3)}


def reference(x, W1, b1, W2, b2, Wf, bf):
    x = f64(x)
    mask = np.mean(np.abs(x), axis=1) > THRESHOLD
    xq = mxq(x, 1, "e4m3")
    o1 = np.maximum((xq @ mxq(f64(W1), 1, "e4m3").T) + f64(b1), 0.0)
    o2 = np.maximum((xq @ mxq(f64(W2), 1, "e4m3").T) + f64(b2), 0.0)
    final_dim = W1.shape[0]
    o2p = np.pad(o2, ((0, 0), (0, final_dim - o2.shape[1])))
    branch_out = np.where(mask[:, None], o1, o2p)
    return (mxq(branch_out, 1, "e4m3") @ mxq(f64(Wf), 1, "e4m3").T) + f64(bf)

@@ -1,0 +1,237 @@
+from contextlib import ExitStack
+
+import concourse.mybir as mybir
+from concourse.masks import make_identity
+
+F32 = mybir.dt.float32
+BF16 = mybir.dt.bfloat16
+U32 = mybir.dt.uint32
+U8 = mybir.dt.uint8
+FP8X4 = mybir.dt.float8_e4m3fn_x4
+ALU = mybir.AluOpType
+ACT = mybir.ActivationFunctionType
+
+P = 128
+H = 64
+B, D, U1, U2 = 8192, 512, 512, 256
+FLOPS = 2 * B * D * (U1 + U2) + 2 * B * U1 * D
+CH = 512
+HC = CH // 2
+NCH = B // CH
+SUP = 1024
+NSUP = B // SUP
+
+
+def tile_dynamiclayer_t_kernel(tc, x, W1, b1, W2, b2, Wf, bf, out):
+    nc = tc.nc
+    with ExitStack() as ctx:
+        const = ctx.enter_context(tc.tile_pool(name="const", bufs=1))
+        xpool = ctx.enter_context(tc.tile_pool(name="xpool", bufs=1))
+        work = ctx.enter_context(tc.tile_pool(name="work", bufs=2))
+        opool = ctx.enter_context(tc.tile_pool(name="opool", bufs=3))
+        ps_x = ctx.enter_context(tc.psum_pool(name="ps_x", bufs=2))
+        ps_z = ctx.enter_context(tc.psum_pool(name="ps_z", bufs=3))
+        ps_y = ctx.enter_context(tc.psum_pool(name="ps_y", bufs=2))
+        ps_m = ctx.enter_context(tc.psum_pool(name="ps_m", bufs=1))
+
+        w1_sb = const.tile([P, 4 * D], BF16)
+        w2_sb = const.tile([P, 4 * D], BF16)
+        wf_sb = const.tile([P, 4 * 2 * U1], BF16)
+        nc.vector.memset(w2_sb[H:P, :], 0.0)
+        nc.sync.dma_start(out=w1_sb[:], in_=W1.rearrange("(m t) k -> m (t k)", t=4))
+        nc.sync.dma_start(out=w2_sb[0:H, :], in_=W2.rearrange("(m t) k -> m (t k)", t=4))
+        x_view = x.rearrange("(s p r) k -> s p (r k)", p=P, r=SUP // P)
+        xs = []
+        for s in range(NSUP):
+            xt_sb = xpool.tile([P, (SUP // P) * D], BF16, name="x%d" % s)
+            xs.append(xt_sb)
+        nc.sync.dma_start(out=xs[0][:], in_=x_view[0])
+        wf_dst = wf_sb[:].rearrange("p (a h u) -> p a h u", a=4, h=2)
+        for h in range(2):
+            nc.sync.dma_start(out=wf_dst[:, :, h, :], in_=Wf.rearrange("(a p) u -> p a u", p=P))
+        for s in range(1, NSUP):
+            nc.sync.dma_start(out=xs[s][:], in_=x_view[s])
+
+        bb1 = const.tile([P, 4], BF16)
+        bb1r = const.tile([P, 4], BF16)
+        bb2 = const.tile([P, 4], BF16)
+        b1v = b1.rearrange("(p t) -> p t", t=4)
+        b2v = b2.rearrange("(p t) -> p t", t=4)
+        with nc.allow_non_contiguous_dma(reason="four bias values to a partition"):
+            nc.scalar.dma_start(out=bb1[:], in_=b1v)
+            nc.scalar.dma_start(out=bb1r[0:H, :], in_=b1v[H:P, :])
+            nc.scalar.dma_start(out=bb1r[H:P, :], in_=b1v[0:H, :])
+            nc.scalar.dma_start(out=bb2[0:H, :], in_=b2v)
+            nc.scalar.dma_start(out=bb2[H:P, :], in_=b2v)
+        bfb = const.tile([P, D], BF16)
+        nc.gpsimd.dma_start(out=bfb[:], in_=bf.partition_broadcast(P))
+
+        ident_f = const.tile([P, P], F32)
+        make_identity(nc, ident_f[:])
+        ident_b = const.tile([P, P], BF16)
+        make_identity(nc, ident_b[:])
+
+        bc1 = const.tile([P, 4], F32)
+        bc1r = const.tile([P, 4], F32)
+        bc2 = const.tile([P, 4], F32)
+        nc.vector.tensor_copy(out=bc1[:], in_=bb1[:])
+        nc.vector.tensor_copy(out=bc1r[:], in_=bb1r[:])
+        nc.vector.tensor_copy(out=bc2[:], in_=bb2[:])
+
+        def bank_of_transposes(srcs, dsts, copy_engine):
+            xt = ps_x.tile([P, 512], F32, tag="xt")
+            for n in range(4):
+                nc.tensor.transpose(xt[:, n * P:(n + 1) * P], srcs[n], ident_f[:])
+            src = xt[:].rearrange("p (r u j) -> p r j u", r=2, u=2)
+            for dst in dsts:
+                if copy_engine == "s":
+                    nc.scalar.copy(out=dst, in_=src)
+                else:
+                    nc.vector.tensor_copy(out=dst, in_=src)
+
+        def halves(src_f32, tile_index):
+            base = tile_index * 256
+            return [src_f32[:, base:base + P], src_f32[:, base + P:base + 2 * P]]
+
+        def stationary(w_sb, engine):
+            g = const.tile([P, 4 * 2 * P * 4], BF16, align_bytes=64, name="g_" + engine)
+            codes = const.tile([P, 4 * 2 * P], U32, align_bytes=64, name="c_" + engine)
+            scales = const.tile([P, 4 * 2 * P], U8, align_bytes=64, name="s_" + engine)
+            gv = g[:].bitcast(F32).rearrange("p (t d j u) -> p t d j u", t=4, d=2, u=2)
+            wv = w_sb[:].bitcast(F32)
+            for q in range(2):
+                bank_of_transposes(halves(wv, 2 * q) + halves(wv, 2 * q + 1),
+                                   [gv[:, 2 * q:2 * q + 2, 0], gv[:, 2 * q:2 * q + 2, 1]], engine)
+            nc.vector.quantize_mx(out=codes[:].bitcast(FP8X4), scales=scales[:], in_=g[:])
+            return codes, scales
+
+        w1c, w1s = stationary(w1_sb, "v")
+        w2c, w2s = stationary(w2_sb, "s")
+
+        def slot(codes, scales, t, shifted):
+            lo = t * 2 * P + (H if shifted else 0)
+            return codes[:, lo:lo + P].bitcast(FP8X4), scales[:, lo:lo + P]
+
+        wfq = []
+
+        def prepare_wf():
+            wv = wf_sb[:].bitcast(F32)
+            for shifted in range(2):
+                g = const.tile([P, D * 4], BF16, align_bytes=64, name="wfg%d" % shifted)
+                codes = const.tile([P, D], U32, align_bytes=64, name="wfc%d" % shifted)
+                scales = const.tile([P, D], U8, align_bytes=64, name="wfs%d" % shifted)
+                gv = g[:].bitcast(F32).rearrange("p (a j u) -> p a j u", a=4, u=2)
+                for q in range(2):
+                    srcs = []
+                    for a in (2 * q, 2 * q + 1):
+                        for u in range(2):
+                            lo = a * 512 + shifted * P + u
+                            srcs.append(wv[:, lo:lo + 256:2])
+                    bank_of_transposes(srcs, [gv[:, 2 * q:2 * q + 2]], "v")
+                nc.vector.quantize_mx(out=codes[:].bitcast(FP8X4), scales=scales[:], in_=g[:])
+                wfq.append((codes, scales))
+
+        state = {}
+
+        def front(c):
+            s, h = c // 2, c % 2
+            xc_sb = xs[s][:, h * 4 * D:(h + 1) * 4 * D]
+            ssum = work.tile([P, 4], F32, tag="ssum")
+            for r in range(4):
+                junk = work.tile([P, D], BF16, tag="junk")
+                nc.scalar.activation(out=junk[:], in_=xc_sb[:, r * D:(r + 1) * D], func=ACT.Abs,
+                                     accum_out=ssum[:, r:r + 1])
+            mcol = work.tile([P, 4], BF16, tag="mcol")
+            nc.vector.tensor_scalar(out=mcol[:], in0=ssum[:], scalar1=float(D), scalar2=None,
+                                    op0=ALU.is_gt)
+            nl = work.tile([P, 2 * P], BF16, tag="nl")
+            nc.vector.tensor_scalar(
+                out=nl[:].rearrange("p (r h c) -> p r h c", r=2, h=2),
+                in0=ssum[:].rearrange("p (h r) -> p r h", h=2).unsqueeze(3).to_broadcast([P, 2, 2, H]),
+                scalar1=float(D), scalar2=None, op0=ALU.is_le)
+            xg = work.tile([P, CH * 4], BF16, tag="xg", align_bytes=64)
+            gv = xg[:].bitcast(F32).rearrange("p (r j u) -> p r j u", r=4, u=2)
+            xv = xc_sb.bitcast(F32)
+            for q in range(2):
+                bank_of_transposes(halves(xv, 2 * q) + halves(xv, 2 * q + 1), [gv[:, 2 * q:2 * q + 2]], "s")
+            xc = work.tile([P, CH], U32, tag="xc", align_bytes=64)
+            xsc = work.tile([P, CH], U8, tag="xsc", align_bytes=64)
+            nc.vector.quantize_mx(out=xc[:].bitcast(FP8X4), scales=xsc[:], in_=xg[:])
+            state[("x", c)] = (xc, xsc, mcol, nl)
+
+        def mid(c):
+            xc, xsc, mcol, nl = state[("x", c)]
+            mb = ps_m.tile([P, CH + HC], BF16, tag="mb")
+            for r in range(4):
+                nc.tensor.matmul(out=mb[:, r * P:(r + 1) * P], lhsT=mcol[:, r:r + 1].to_broadcast([P, P]),
+                                 rhs=ident_b[:], start=True, stop=True)
+            for r in range(2):
+                nc.tensor.matmul(out=mb[:, CH + r * P:CH + (r + 1) * P], lhsT=nl[:, r * P:(r + 1) * P],
+                                 rhs=ident_b[:], start=True, stop=True)
+            half = [(xc[:, g * HC:(g + 1) * HC].bitcast(FP8X4), xsc[:, g * HC:(g + 1) * HC]) for g in range(2)]
+            r1 = work.tile([P, 4 * CH], BF16, tag="r1")
+            r2 = work.tile([P, 4 * HC], BF16, tag="r2")
+            for t in range(4):
+                z = ps_z.tile([P, CH], F32, tag="z")
+                for g in range(2):
+                    wc, ws = slot(w1c, w1s, t, g == 1)
+                    nc.tensor.matmul_mx(out=z[:, g * HC:(g + 1) * HC], lhsT=wc, lhsT_scale=ws,
+                                        rhs=half[g][0], rhs_scale=half[g][1], start=True, stop=True)
+                for g in range(2):
+                    bias = bc1r if g == 1 else bc1
+                    nc.scalar.activation(out=r1[:, t * CH + g * HC:t * CH + (g + 1) * HC],
+                                         in_=z[:, g * HC:(g + 1) * HC], func=ACT.Relu,
+                                         bias=bias[:, t:t + 1], scale=1.0)
+            for q in range(2):
+                z = ps_z.tile([P, CH], F32, tag="z")
+                for tt in range(2):
+                    t = 2 * q + tt
+                    for g in range(2):
+                        wc, ws = slot(w2c, w2s, t, g == 1)
+                        nc.tensor.matmul_mx(out=z[:, tt * HC:(tt + 1) * HC], lhsT=wc, lhsT_scale=ws,
+                                            rhs=half[g][0], rhs_scale=half[g][1],
+                                            start=(g == 0), stop=(g == 1))
+                for tt in range(2):
+                    t = 2 * q + tt
+                    nc.scalar.activation(out=r2[:, t * HC:(t + 1) * HC], in_=z[:, tt * HC:(tt + 1) * HC],
+                                         func=ACT.Relu, bias=bc2[:, t:t + 1], scale=1.0)
+            r1v = r1[:].rearrange("p (t i) -> p t i", t=4)
+            r2v = r2[:].rearrange("p (t i) -> p t i", t=4)
+            nc.vector.tensor_tensor(out=r2v, in0=r2v,
+                                    in1=mb[:, CH:CH + HC].unsqueeze(1).to_broadcast([P, 4, HC]), op=ALU.mult)
+            nc.vector.tensor_tensor(out=r1v, in0=r1v,
+                                    in1=mb[:, 0:CH].unsqueeze(1).to_broadcast([P, 4, CH]), op=ALU.mult)
+            nc.vector.tensor_tensor(out=r1v[0:H, :, 0:HC], in0=r1v[0:H, :, 0:HC], in1=r2v[0:H], op=ALU.max)
+            nc.vector.tensor_tensor(out=r1v[H:P, :, HC:CH], in0=r1v[H:P, :, HC:CH], in1=r2v[H:P], op=ALU.max)
+            hg = work.tile([P, CH * 4], BF16, tag="hg", align_bytes=64)
+            nc.vector.tensor_copy(out=hg[:].rearrange("p (c i t) -> p c t i", i=4, t=4),
+                                  in_=r1[:].rearrange("p (t c i) -> p c t i", t=4, i=4))
+            hc = work.tile([P, CH], U32, tag="hc", align_bytes=64)
+            hs = work.tile([P, CH], U8, tag="hs", align_bytes=64)
+            nc.vector.quantize_mx(out=hc[:].bitcast(FP8X4), scales=hs[:], in_=hg[:])
+            state[("h", c)] = (hc, hs)
+
+        out_view = out.rearrange("(s p r) d -> s p (r d)", p=P, r=SUP // P)
+
+        def back(c):
+            s, h = c // 2, c % 2
+            hc, hs = state[("h", c)]
+            osb = opool.tile([P, 4 * D], F32, tag="osb")
+            for r in range(4):
+                wc, ws = wfq[r // 2]
+                y = ps_y.tile([P, D], F32, tag="y")
+                nc.tensor.matmul_mx(out=y[:], lhsT=hc[:, r * P:(r + 1) * P].bitcast(FP8X4),
+                                    lhsT_scale=hs[:, r * P:(r + 1) * P],
+                                    rhs=wc[:].bitcast(FP8X4), rhs_scale=ws[:], start=True, stop=True)
+                nc.vector.tensor_tensor(out=osb[:, r * D:(r + 1) * D], in0=y[:], in1=bfb[:], op=ALU.add)
+            nc.sync.dma_start(out=out_view[s][:, h * 4 * D:(h + 1) * 4 * D], in_=osb[:])
+
+        for c in range(NCH + 2):
+            if c >= 2:
+                back(c - 2)
+            if c < NCH:
+                front(c)
+            if c == 0:
+                prepare_wf()
+            if 1 <= c <= NCH:
+                mid(c - 1)

@@ -204,8 +204,9 @@ def tile_dynamiclayer_t_kernel(tc, x, W1, b1, W2, b2, Wf, bf, out):
             nc.vector.tensor_tensor(out=r1v[0:H, :, 0:HC], in0=r1v[0:H, :, 0:HC], in1=r2v[0:H], op=ALU.max)
             nc.vector.tensor_tensor(out=r1v[H:P, :, HC:CH], in0=r1v[H:P, :, HC:CH], in1=r2v[H:P], op=ALU.max)
             hg = work.tile([P, CH * 4], BF16, tag="hg", align_bytes=64)
-            nc.vector.tensor_copy(out=hg[:].rearrange("p (c i t) -> p c t i", i=4, t=4),
-                                  in_=r1[:].rearrange("p (t c i) -> p c t i", t=4, i=4))
+            nc.gpsimd.tensor_scalar(out=hg[:].rearrange("p (i t) -> p i t", t=4),
+                                    in0=r1[:].rearrange("p (t i) -> p i t", t=4),
+                                    scalar1=1.0, scalar2=0.0, op0=ALU.mult, op1=ALU.add)
             hc = work.tile([P, CH], U32, tag="hc", align_bytes=64)
             hs = work.tile([P, CH], U8, tag="hs", align_bytes=64)
             nc.vector.quantize_mx(out=hc[:].bitcast(FP8X4), scales=hs[:], in_=hg[:])

@@ -17,6 +17,7 @@ B, D, U1, U2 = 8192, 512, 512, 256
 FLOPS = 2 * B * D * (U1 + U2) + 2 * B * U1 * D
 CH = 512
 HC = CH // 2
+SL = CH + HC
 NCH = B // CH
 SUP = 1024
 NSUP = B // SUP
@@ -142,10 +143,10 @@ def tile_dynamiclayer_t_kernel(tc, x, W1, b1, W2, b2, Wf, bf, out):
                 nc.scalar.activation(out=junk[:], in_=xc_sb[:, r * D:(r + 1) * D], func=ACT.Abs,
                                      accum_out=ssum[:, r:r + 1])
             mcol = work.tile([P, 4], BF16, tag="mcol")
-            nc.vector.tensor_scalar(out=mcol[:], in0=ssum[:], scalar1=float(D), scalar2=None,
+            nc.gpsimd.tensor_scalar(out=mcol[:], in0=ssum[:], scalar1=float(D), scalar2=None,
                                     op0=ALU.is_gt)
             nl = work.tile([P, 2 * P], BF16, tag="nl")
-            nc.vector.tensor_scalar(
+            nc.gpsimd.tensor_scalar(
                 out=nl[:].rearrange("p (r h c) -> p r h c", r=2, h=2),
                 in0=ssum[:].rearrange("p (h r) -> p r h", h=2).unsqueeze(3).to_broadcast([P, 2, 2, H]),
                 scalar1=float(D), scalar2=None, op0=ALU.is_le)
@@ -169,8 +170,7 @@ def tile_dynamiclayer_t_kernel(tc, x, W1, b1, W2, b2, Wf, bf, out):
                 nc.tensor.matmul(out=mb[:, CH + r * P:CH + (r + 1) * P], lhsT=nl[:, r * P:(r + 1) * P],
                                  rhs=ident_b[:], start=True, stop=True)
             half = [(xc[:, g * HC:(g + 1) * HC].bitcast(FP8X4), xsc[:, g * HC:(g + 1) * HC]) for g in range(2)]
-            r1 = work.tile([P, 4 * CH], BF16, tag="r1")
-            r2 = work.tile([P, 4 * HC], BF16, tag="r2")
+            rr = work.tile([P, 4 * SL], BF16, tag="rr")
             for t in range(4):
                 z = ps_z.tile([P, CH], F32, tag="z")
                 for g in range(2):
@@ -179,7 +179,7 @@ def tile_dynamiclayer_t_kernel(tc, x, W1, b1, W2, b2, Wf, bf, out):
                                         rhs=half[g][0], rhs_scale=half[g][1], start=True, stop=True)
                 for g in range(2):
                     bias = bc1r if g == 1 else bc1
-                    nc.scalar.activation(out=r1[:, t * CH + g * HC:t * CH + (g + 1) * HC],
+                    nc.scalar.activation(out=rr[:, t * SL + g * HC:t * SL + (g + 1) * HC],
                                          in_=z[:, g * HC:(g + 1) * HC], func=ACT.Relu,
                                          bias=bias[:, t:t + 1], scale=1.0)
             for q in range(2):
@@ -193,20 +193,17 @@ def tile_dynamiclayer_t_kernel(tc, x, W1, b1, W2, b2, Wf, bf, out):
                                             start=(g == 0), stop=(g == 1))
                 for tt in range(2):
                     t = 2 * q + tt
-                    nc.scalar.activation(out=r2[:, t * HC:(t + 1) * HC], in_=z[:, tt * HC:(tt + 1) * HC],
+                    nc.scalar.activation(out=rr[:, t * SL + CH:(t + 1) * SL], in_=z[:, tt * HC:(tt + 1) * HC],
                                          func=ACT.Relu, bias=bc2[:, t:t + 1], scale=1.0)
-            r1v = r1[:].rearrange("p (t i) -> p t i", t=4)
-            r2v = r2[:].rearrange("p (t i) -> p t i", t=4)
-            nc.vector.tensor_tensor(out=r2v, in0=r2v,
-                                    in1=mb[:, CH:CH + HC].unsqueeze(1).to_broadcast([P, 4, HC]), op=ALU.mult)
-            nc.vector.tensor_tensor(out=r1v, in0=r1v,
-                                    in1=mb[:, 0:CH].unsqueeze(1).to_broadcast([P, 4, CH]), op=ALU.mult)
-            nc.vector.tensor_tensor(out=r1v[0:H, :, 0:HC], in0=r1v[0:H, :, 0:HC], in1=r2v[0:H], op=ALU.max)
-            nc.vector.tensor_tensor(out=r1v[H:P, :, HC:CH], in0=r1v[H:P, :, HC:CH], in1=r2v[H:P], op=ALU.max)
+            rv = rr[:].rearrange("p (t i) -> p t i", t=4)
+            nc.vector.tensor_tensor(out=rv, in0=rv, in1=mb[:].unsqueeze(1).to_broadcast([P, 4, SL]), op=ALU.mult)
+            nc.vector.tensor_tensor(out=rv[0:H, :, 0:HC], in0=rv[0:H, :, 0:HC], in1=rv[0:H, :, CH:SL], op=ALU.max)
+            nc.vector.tensor_tensor(out=rv[H:P, :, HC:CH], in0=rv[H:P, :, HC:CH], in1=rv[H:P, :, CH:SL], op=ALU.max)
             hg = work.tile([P, CH * 4], BF16, tag="hg", align_bytes=64)
-            nc.gpsimd.tensor_scalar(out=hg[:].rearrange("p (i t) -> p i t", t=4),
-                                    in0=r1[:].rearrange("p (t i) -> p i t", t=4),
-                                    scalar1=1.0, scalar2=0.0, op0=ALU.mult, op1=ALU.add)
+            nc.vector.tensor_copy(out=hg[:, 0:384 * 4].rearrange("p (c i t) -> p c t i", i=4, t=4),
+                                  in_=rv[:, :, 0:384].rearrange("p t (c i) -> p c t i", i=4))
+            nc.scalar.copy(out=hg[:, 384 * 4:CH * 4].rearrange("p (c i t) -> p c t i", i=4, t=4),
+                           in_=rv[:, :, 384:CH].rearrange("p t (c i) -> p c t i", i=4))
             hc = work.tile([P, CH], U32, tag="hc", align_bytes=64)
             hs = work.tile([P, CH], U8, tag="hs", align_bytes=64)
             nc.vector.quantize_mx(out=hc[:].bitcast(FP8X4), scales=hs[:], in_=hg[:])
@@ -225,7 +222,11 @@ def tile_dynamiclayer_t_kernel(tc, x, W1, b1, W2, b2, Wf, bf, out):
                                     lhsT_scale=hs[:, r * P:(r + 1) * P],
                                     rhs=wc[:].bitcast(FP8X4), rhs_scale=ws[:], start=True, stop=True)
                 nc.vector.tensor_tensor(out=osb[:, r * D:(r + 1) * D], in0=y[:], in1=bfb[:], op=ALU.add)
-            nc.sync.dma_start(out=out_view[s][:, h * 4 * D:(h + 1) * 4 * D], in_=osb[:])
+            pieces = 4 if c == NCH - 1 else 1
+            w = 4 * D // pieces
+            for e in range(pieces):
+                nc.sync.dma_start(out=out_view[s][:, h * 4 * D + e * w:h * 4 * D + (e + 1) * w],
+                                  in_=osb[:, e * w:(e + 1) * w])
 
         for c in range(NCH + 2):
             if c >= 2:

@@ -21,6 +21,9 @@ SL = CH + HC
 NCH = B // CH
 SUP = 1024
 NSUP = B // SUP
+AX = mybir.AxisListType
+SUM_ON_VECTOR = ()
+REGROUP_ON_VECTOR = (0,1,2,3,4,5,6,7,8,9,10,11,12,13,14,15)
 
 
 def tile_dynamiclayer_t_kernel(tc, x, W1, b1, W2, b2, Wf, bf, out):
@@ -64,20 +67,16 @@ def tile_dynamiclayer_t_kernel(tc, x, W1, b1, W2, b2, Wf, bf, out):
             nc.scalar.dma_start(out=bb1r[H:P, :], in_=b1v[0:H, :])
             nc.scalar.dma_start(out=bb2[0:H, :], in_=b2v)
             nc.scalar.dma_start(out=bb2[H:P, :], in_=b2v)
-        bfb = const.tile([P, D], BF16)
-        nc.gpsimd.dma_start(out=bfb[:], in_=bf.partition_broadcast(P))
-
         ident_f = const.tile([P, P], F32)
         make_identity(nc, ident_f[:])
         ident_b = const.tile([P, P], BF16)
         make_identity(nc, ident_b[:])
+        bfb = const.tile([P, D], BF16)
+        nc.gpsimd.dma_start(out=bfb[:], in_=bf.partition_broadcast(P))
 
         bc1 = const.tile([P, 4], F32)
         bc1r = const.tile([P, 4], F32)
         bc2 = const.tile([P, 4], F32)
-        nc.vector.tensor_copy(out=bc1[:], in_=bb1[:])
-        nc.vector.tensor_copy(out=bc1r[:], in_=bb1r[:])
-        nc.vector.tensor_copy(out=bc2[:], in_=bb2[:])
 
         def bank_of_transposes(srcs, dsts, copy_engine):
             xt = ps_x.tile([P, 512], F32, tag="xt")
@@ -108,6 +107,9 @@ def tile_dynamiclayer_t_kernel(tc, x, W1, b1, W2, b2, Wf, bf, out):
 
         w1c, w1s = stationary(w1_sb, "v")
         w2c, w2s = stationary(w2_sb, "s")
+        nc.vector.tensor_copy(out=bc1[:], in_=bb1[:])
+        nc.vector.tensor_copy(out=bc1r[:], in_=bb1r[:])
+        nc.vector.tensor_copy(out=bc2[:], in_=bb2[:])
 
         def slot(codes, scales, t, shifted):
             lo = t * 2 * P + (H if shifted else 0)
@@ -134,14 +136,24 @@ def tile_dynamiclayer_t_kernel(tc, x, W1, b1, W2, b2, Wf, bf, out):
 
         state = {}
 
-        def front(c):
-            s, h = c // 2, c % 2
-            xc_sb = xs[s][:, h * 4 * D:(h + 1) * 4 * D]
+        def rows_of(c):
+            return xs[c // 2][:, (c % 2) * 4 * D:(c % 2 + 1) * 4 * D]
+
+        def step_sum(c):
+            xc_sb = rows_of(c)
             ssum = work.tile([P, 4], F32, tag="ssum")
-            for r in range(4):
-                junk = work.tile([P, D], BF16, tag="junk")
-                nc.scalar.activation(out=junk[:], in_=xc_sb[:, r * D:(r + 1) * D], func=ACT.Abs,
-                                     accum_out=ssum[:, r:r + 1])
+            if c in SUM_ON_VECTOR:
+                nc.vector.tensor_reduce(out=ssum[:], in_=xc_sb.rearrange("p (r k) -> p r k", r=4), axis=AX.X,
+                                        op=ALU.add, apply_absolute_value=True)
+            else:
+                for r in range(4):
+                    junk = work.tile([P, D], BF16, tag="junk")
+                    nc.scalar.activation(out=junk[:], in_=xc_sb[:, r * D:(r + 1) * D], func=ACT.Abs,
+                                         accum_out=ssum[:, r:r + 1])
+            state[("sum", c)] = ssum
+
+        def step_compare(c):
+            ssum = state[("sum", c)]
             mcol = work.tile([P, 4], BF16, tag="mcol")
             nc.gpsimd.tensor_scalar(out=mcol[:], in0=ssum[:], scalar1=float(D), scalar2=None,
                                     op0=ALU.is_gt)
@@ -150,18 +162,35 @@ def tile_dynamiclayer_t_kernel(tc, x, W1, b1, W2, b2, Wf, bf, out):
                 out=nl[:].rearrange("p (r h c) -> p r h c", r=2, h=2),
                 in0=ssum[:].rearrange("p (h r) -> p r h", h=2).unsqueeze(3).to_broadcast([P, 2, 2, H]),
                 scalar1=float(D), scalar2=None, op0=ALU.is_le)
+            state[("cmp", c)] = (mcol, nl)
+
+        def step_transpose(c):
+            xv = rows_of(c).bitcast(F32)
+            banks = []
+            for q in range(2):
+                xt = ps_x.tile([P, 512], F32, tag="xt")
+                srcs = halves(xv, 2 * q) + halves(xv, 2 * q + 1)
+                for n in range(4):
+                    nc.tensor.transpose(xt[:, n * P:(n + 1) * P], srcs[n], ident_f[:])
+                banks.append(xt)
+            state[("xt", c)] = banks
+
+        def step_copy_x(c):
             xg = work.tile([P, CH * 4], BF16, tag="xg", align_bytes=64)
             gv = xg[:].bitcast(F32).rearrange("p (r j u) -> p r j u", r=4, u=2)
-            xv = xc_sb.bitcast(F32)
             for q in range(2):
-                bank_of_transposes(halves(xv, 2 * q) + halves(xv, 2 * q + 1), [gv[:, 2 * q:2 * q + 2]], "s")
+                nc.scalar.copy(out=gv[:, 2 * q:2 * q + 2],
+                               in_=state[("xt", c)][q][:].rearrange("p (r u j) -> p r j u", r=2, u=2))
+            state[("xg", c)] = xg
+
+        def step_quantise_x(c):
             xc = work.tile([P, CH], U32, tag="xc", align_bytes=64)
             xsc = work.tile([P, CH], U8, tag="xsc", align_bytes=64)
-            nc.vector.quantize_mx(out=xc[:].bitcast(FP8X4), scales=xsc[:], in_=xg[:])
-            state[("x", c)] = (xc, xsc, mcol, nl)
+            nc.vector.quantize_mx(out=xc[:].bitcast(FP8X4), scales=xsc[:], in_=state[("xg", c)][:])
+            state[("x", c)] = (xc, xsc)
 
-        def mid(c):
-            xc, xsc, mcol, nl = state[("x", c)]
+        def step_spread_masks(c):
+            mcol, nl = state[("cmp", c)]
             mb = ps_m.tile([P, CH + HC], BF16, tag="mb")
             for r in range(4):
                 nc.tensor.matmul(out=mb[:, r * P:(r + 1) * P], lhsT=mcol[:, r:r + 1].to_broadcast([P, P]),
@@ -169,6 +198,10 @@ def tile_dynamiclayer_t_kernel(tc, x, W1, b1, W2, b2, Wf, bf, out):
             for r in range(2):
                 nc.tensor.matmul(out=mb[:, CH + r * P:CH + (r + 1) * P], lhsT=nl[:, r * P:(r + 1) * P],
                                  rhs=ident_b[:], start=True, stop=True)
+            state[("mb", c)] = mb
+
+        def step_hidden(c):
+            xc, xsc = state[("x", c)]
             half = [(xc[:, g * HC:(g + 1) * HC].bitcast(FP8X4), xsc[:, g * HC:(g + 1) * HC]) for g in range(2)]
             rr = work.tile([P, 4 * SL], BF16, tag="rr")
             for t in range(4):
@@ -195,23 +228,33 @@ def tile_dynamiclayer_t_kernel(tc, x, W1, b1, W2, b2, Wf, bf, out):
                     t = 2 * q + tt
                     nc.scalar.activation(out=rr[:, t * SL + CH:(t + 1) * SL], in_=z[:, tt * HC:(tt + 1) * HC],
                                          func=ACT.Relu, bias=bc2[:, t:t + 1], scale=1.0)
-            rv = rr[:].rearrange("p (t i) -> p t i", t=4)
+            state[("r", c)] = rr
+
+        def step_select(c):
+            rv = state[("r", c)][:].rearrange("p (t i) -> p t i", t=4)
+            mb = state[("mb", c)]
             nc.vector.tensor_tensor(out=rv, in0=rv, in1=mb[:].unsqueeze(1).to_broadcast([P, 4, SL]), op=ALU.mult)
             nc.vector.tensor_tensor(out=rv[0:H, :, 0:HC], in0=rv[0:H, :, 0:HC], in1=rv[0:H, :, CH:SL], op=ALU.max)
             nc.vector.tensor_tensor(out=rv[H:P, :, HC:CH], in0=rv[H:P, :, HC:CH], in1=rv[H:P, :, CH:SL], op=ALU.max)
+
+        def step_regroup(c):
+            rv = state[("r", c)][:].rearrange("p (t i) -> p t i", t=4)
             hg = work.tile([P, CH * 4], BF16, tag="hg", align_bytes=64)
             nc.vector.tensor_copy(out=hg[:, 0:384 * 4].rearrange("p (c i t) -> p c t i", i=4, t=4),
                                   in_=rv[:, :, 0:384].rearrange("p t (c i) -> p c t i", i=4))
             nc.scalar.copy(out=hg[:, 384 * 4:CH * 4].rearrange("p (c i t) -> p c t i", i=4, t=4),
                            in_=rv[:, :, 384:CH].rearrange("p t (c i) -> p c t i", i=4))
+            state[("hg", c)] = hg
+
+        def step_quantise_h(c):
             hc = work.tile([P, CH], U32, tag="hc", align_bytes=64)
             hs = work.tile([P, CH], U8, tag="hs", align_bytes=64)
-            nc.vector.quantize_mx(out=hc[:].bitcast(FP8X4), scales=hs[:], in_=hg[:])
+            nc.vector.quantize_mx(out=hc[:].bitcast(FP8X4), scales=hs[:], in_=state[("hg", c)][:])
             state[("h", c)] = (hc, hs)
 
         out_view = out.rearrange("(s p r) d -> s p (r d)", p=P, r=SUP // P)
 
-        def back(c):
+        def step_output(c):
             s, h = c // 2, c % 2
             hc, hs = state[("h", c)]
             osb = opool.tile([P, 4 * D], F32, tag="osb")
@@ -222,18 +265,34 @@ def tile_dynamiclayer_t_kernel(tc, x, W1, b1, W2, b2, Wf, bf, out):
                                     lhsT_scale=hs[:, r * P:(r + 1) * P],
                                     rhs=wc[:].bitcast(FP8X4), rhs_scale=ws[:], start=True, stop=True)
                 nc.vector.tensor_tensor(out=osb[:, r * D:(r + 1) * D], in0=y[:], in1=bfb[:], op=ALU.add)
-            pieces = 4 if c == NCH - 1 else 1
-            w = 4 * D // pieces
-            for e in range(pieces):
-                nc.sync.dma_start(out=out_view[s][:, h * 4 * D + e * w:h * 4 * D + (e + 1) * w],
-                                  in_=osb[:, e * w:(e + 1) * w])
+                if c == NCH - 1:
+                    nc.sync.dma_start(out=out_view[s][:, (h * 4 + r) * D:(h * 4 + r + 1) * D],
+                                      in_=osb[:, r * D:(r + 1) * D])
+            if c != NCH - 1:
+                nc.sync.dma_start(out=out_view[s][:, h * 4 * D:(h + 1) * 4 * D], in_=osb[:])
 
-        for c in range(NCH + 2):
-            if c >= 2:
-                back(c - 2)
-            if c < NCH:
-                front(c)
-            if c == 0:
+        def live(c):
+            return 0 <= c < NCH
+
+        for n in range(-2, NCH + 2):
+            if live(n - 2):
+                step_quantise_h(n - 2)
+            if live(n + 1):
+                step_compare(n + 1)
+                step_copy_x(n + 1)
+            if live(n - 1):
+                step_select(n - 1)
+                step_regroup(n - 1)
+            if live(n):
+                step_hidden(n)
+            if live(n + 1):
+                step_quantise_x(n + 1)
+            if live(n):
+                step_spread_masks(n)
+            if n == 0:
                 prepare_wf()
-            if 1 <= c <= NCH:
-                mid(c - 1)
+            if live(n + 2):
+                step_transpose(n + 2)
+                step_sum(n + 2)
+            if live(n - 2):
+                step_output(n - 2)

@@ -21,9 +21,6 @@ SL = CH + HC
 NCH = B // CH
 SUP = 1024
 NSUP = B // SUP
-AX = mybir.AxisListType
-SUM_ON_VECTOR = ()
-REGROUP_ON_VECTOR = (0,1,2,3,4,5,6,7,8,9,10,11,12,13,14,15)
 
 
 def tile_dynamiclayer_t_kernel(tc, x, W1, b1, W2, b2, Wf, bf, out):
@@ -67,16 +64,20 @@ def tile_dynamiclayer_t_kernel(tc, x, W1, b1, W2, b2, Wf, bf, out):
             nc.scalar.dma_start(out=bb1r[H:P, :], in_=b1v[0:H, :])
             nc.scalar.dma_start(out=bb2[0:H, :], in_=b2v)
             nc.scalar.dma_start(out=bb2[H:P, :], in_=b2v)
+        bfb = const.tile([P, D], BF16)
+        nc.gpsimd.dma_start(out=bfb[:], in_=bf.partition_broadcast(P))
+
         ident_f = const.tile([P, P], F32)
         make_identity(nc, ident_f[:])
         ident_b = const.tile([P, P], BF16)
         make_identity(nc, ident_b[:])
-        bfb = const.tile([P, D], BF16)
-        nc.gpsimd.dma_start(out=bfb[:], in_=bf.partition_broadcast(P))
 
         bc1 = const.tile([P, 4], F32)
         bc1r = const.tile([P, 4], F32)
         bc2 = const.tile([P, 4], F32)
+        nc.vector.tensor_copy(out=bc1[:], in_=bb1[:])
+        nc.vector.tensor_copy(out=bc1r[:], in_=bb1r[:])
+        nc.vector.tensor_copy(out=bc2[:], in_=bb2[:])
 
         def bank_of_transposes(srcs, dsts, copy_engine):
             xt = ps_x.tile([P, 512], F32, tag="xt")
@@ -107,9 +108,6 @@ def tile_dynamiclayer_t_kernel(tc, x, W1, b1, W2, b2, Wf, bf, out):
 
         w1c, w1s = stationary(w1_sb, "v")
         w2c, w2s = stationary(w2_sb, "s")
-        nc.vector.tensor_copy(out=bc1[:], in_=bb1[:])
-        nc.vector.tensor_copy(out=bc1r[:], in_=bb1r[:])
-        nc.vector.tensor_copy(out=bc2[:], in_=bb2[:])
 
         def slot(codes, scales, t, shifted):
             lo = t * 2 * P + (H if shifted else 0)
@@ -136,24 +134,14 @@ def tile_dynamiclayer_t_kernel(tc, x, W1, b1, W2, b2, Wf, bf, out):
 
         state = {}
 
-        def rows_of(c):
-            return xs[c // 2][:, (c % 2) * 4 * D:(c % 2 + 1) * 4 * D]
-
-        def step_sum(c):
-            xc_sb = rows_of(c)
+        def front(c):
+            s, h = c // 2, c % 2
+            xc_sb = xs[s][:, h * 4 * D:(h + 1) * 4 * D]
             ssum = work.tile([P, 4], F32, tag="ssum")
-            if c in SUM_ON_VECTOR:
-                nc.vector.tensor_reduce(out=ssum[:], in_=xc_sb.rearrange("p (r k) -> p r k", r=4), axis=AX.X,
-                                        op=ALU.add, apply_absolute_value=True)
-            else:
-                for r in range(4):
-                    junk = work.tile([P, D], BF16, tag="junk")
-                    nc.scalar.activation(out=junk[:], in_=xc_sb[:, r * D:(r + 1) * D], func=ACT.Abs,
-                                         accum_out=ssum[:, r:r + 1])
-            state[("sum", c)] = ssum
-
-        def step_compare(c):
-            ssum = state[("sum", c)]
+            for r in range(4):
+                junk = work.tile([P, D], BF16, tag="junk")
+                nc.scalar.activation(out=junk[:], in_=xc_sb[:, r * D:(r + 1) * D], func=ACT.Abs,
+                                     accum_out=ssum[:, r:r + 1])
             mcol = work.tile([P, 4], BF16, tag="mcol")
             nc.gpsimd.tensor_scalar(out=mcol[:], in0=ssum[:], scalar1=float(D), scalar2=None,
                                     op0=ALU.is_gt)
@@ -162,35 +150,18 @@ def tile_dynamiclayer_t_kernel(tc, x, W1, b1, W2, b2, Wf, bf, out):
                 out=nl[:].rearrange("p (r h c) -> p r h c", r=2, h=2),
                 in0=ssum[:].rearrange("p (h r) -> p r h", h=2).unsqueeze(3).to_broadcast([P, 2, 2, H]),
                 scalar1=float(D), scalar2=None, op0=ALU.is_le)
-            state[("cmp", c)] = (mcol, nl)
-
-        def step_transpose(c):
-            xv = rows_of(c).bitcast(F32)
-            banks = []
-            for q in range(2):
-                xt = ps_x.tile([P, 512], F32, tag="xt")
-                srcs = halves(xv, 2 * q) + halves(xv, 2 * q + 1)
-                for n in range(4):
-                    nc.tensor.transpose(xt[:, n * P:(n + 1) * P], srcs[n], ident_f[:])
-                banks.append(xt)
-            state[("xt", c)] = banks
-
-        def step_copy_x(c):
             xg = work.tile([P, CH * 4], BF16, tag="xg", align_bytes=64)
             gv = xg[:].bitcast(F32).rearrange("p (r j u) -> p r j u", r=4, u=2)
+            xv = xc_sb.bitcast(F32)
             for q in range(2):
-                nc.scalar.copy(out=gv[:, 2 * q:2 * q + 2],
-                               in_=state[("xt", c)][q][:].rearrange("p (r u j) -> p r j u", r=2, u=2))
-            state[("xg", c)] = xg
-
-        def step_quantise_x(c):
+                bank_of_transposes(halves(xv, 2 * q) + halves(xv, 2 * q + 1), [gv[:, 2 * q:2 * q + 2]], "s")
             xc = work.tile([P, CH], U32, tag="xc", align_bytes=64)
             xsc = work.tile([P, CH], U8, tag="xsc", align_bytes=64)
-            nc.vector.quantize_mx(out=xc[:].bitcast(FP8X4), scales=xsc[:], in_=state[("xg", c)][:])
-            state[("x", c)] = (xc, xsc)
+            nc.vector.quantize_mx(out=xc[:].bitcast(FP8X4), scales=xsc[:], in_=xg[:])
+            state[("x", c)] = (xc, xsc, mcol, nl)
 
-        def step_spread_masks(c):
-            mcol, nl = state[("cmp", c)]
+        def mid(c):
+            xc, xsc, mcol, nl = state[("x", c)]
             mb = ps_m.tile([P, CH + HC], BF16, tag="mb")
             for r in range(4):
                 nc.tensor.matmul(out=mb[:, r * P:(r + 1) * P], lhsT=mcol[:, r:r + 1].to_broadcast([P, P]),
@@ -198,10 +169,6 @@ def tile_dynamiclayer_t_kernel(tc, x, W1, b1, W2, b2, Wf, bf, out):
             for r in range(2):
                 nc.tensor.matmul(out=mb[:, CH + r * P:CH + (r + 1) * P], lhsT=nl[:, r * P:(r + 1) * P],
                                  rhs=ident_b[:], start=True, stop=True)
-            state[("mb", c)] = mb
-
-        def step_hidden(c):
-            xc, xsc = state[("x", c)]
             half = [(xc[:, g * HC:(g + 1) * HC].bitcast(FP8X4), xsc[:, g * HC:(g + 1) * HC]) for g in range(2)]
             rr = work.tile([P, 4 * SL], BF16, tag="rr")
             for t in range(4):
@@ -228,33 +195,21 @@ def tile_dynamiclayer_t_kernel(tc, x, W1, b1, W2, b2, Wf, bf, out):
                     t = 2 * q + tt
                     nc.scalar.activation(out=rr[:, t * SL + CH:(t + 1) * SL], in_=z[:, tt * HC:(tt + 1) * HC],
                                          func=ACT.Relu, bias=bc2[:, t:t + 1], scale=1.0)
-            state[("r", c)] = rr
-
-        def step_select(c):
-            rv = state[("r", c)][:].rearrange("p (t i) -> p t i", t=4)
-            mb = state[("mb", c)]
+            rv = rr[:].rearrange("p (t i) -> p t i", t=4)
             nc.vector.tensor_tensor(out=rv, in0=rv, in1=mb[:].unsqueeze(1).to_broadcast([P, 4, SL]), op=ALU.mult)
             nc.vector.tensor_tensor(out=rv[0:H, :, 0:HC], in0=rv[0:H, :, 0:HC], in1=rv[0:H, :, CH:SL], op=ALU.max)
             nc.vector.tensor_tensor(out=rv[H:P, :, HC:CH], in0=rv[H:P, :, HC:CH], in1=rv[H:P, :, CH:SL], op=ALU.max)
-
-        def step_regroup(c):
-            rv = state[("r", c)][:].rearrange("p (t i) -> p t i", t=4)
             hg = work.tile([P, CH * 4], BF16, tag="hg", align_bytes=64)
-            nc.vector.tensor_copy(out=hg[:, 0:384 * 4].rearrange("p (c i t) -> p c t i", i=4, t=4),
-                                  in_=rv[:, :, 0:384].rearrange("p t (c i) -> p c t i", i=4))
-            nc.scalar.copy(out=hg[:, 384 * 4:CH * 4].rearrange("p (c i t) -> p c t i", i=4, t=4),
-                           in_=rv[:, :, 384:CH].rearrange("p t (c i) -> p c t i", i=4))
-            state[("hg", c)] = hg
-
-        def step_quantise_h(c):
+            nc.vector.tensor_copy(out=hg[:, 0:512 * 4].rearrange("p (c i t) -> p c t i", i=4, t=4),
+                                  in_=rv[:, :, 0:512].rearrange("p t (c i) -> p c t i", i=4))
             hc = work.tile([P, CH], U32, tag="hc", align_bytes=64)
             hs = work.tile([P, CH], U8, tag="hs", align_bytes=64)
-            nc.vector.quantize_mx(out=hc[:].bitcast(FP8X4), scales=hs[:], in_=state[("hg", c)][:])
+            nc.vector.quantize_mx(out=hc[:].bitcast(FP8X4), scales=hs[:], in_=hg[:])
             state[("h", c)] = (hc, hs)
 
         out_view = out.rearrange("(s p r) d -> s p (r d)", p=P, r=SUP // P)
 
-        def step_output(c):
+        def back(c):
             s, h = c // 2, c % 2
             hc, hs = state[("h", c)]
             osb = opool.tile([P, 4 * D], F32, tag="osb")
@@ -265,34 +220,18 @@ def tile_dynamiclayer_t_kernel(tc, x, W1, b1, W2, b2, Wf, bf, out):
                                     lhsT_scale=hs[:, r * P:(r + 1) * P],
                                     rhs=wc[:].bitcast(FP8X4), rhs_scale=ws[:], start=True, stop=True)
                 nc.vector.tensor_tensor(out=osb[:, r * D:(r + 1) * D], in0=y[:], in1=bfb[:], op=ALU.add)
-                if c == NCH - 1:
-                    nc.sync.dma_start(out=out_view[s][:, (h * 4 + r) * D:(h * 4 + r + 1) * D],
-                                      in_=osb[:, r * D:(r + 1) * D])
-            if c != NCH - 1:
-                nc.sync.dma_start(out=out_view[s][:, h * 4 * D:(h + 1) * 4 * D], in_=osb[:])
+            pieces = 4 if c == NCH - 1 else 1
+            w = 4 * D // pieces
+            for e in range(pieces):
+                nc.sync.dma_start(out=out_view[s][:, h * 4 * D + e * w:h * 4 * D + (e + 1) * w],
+                                  in_=osb[:, e * w:(e + 1) * w])
 
-        def live(c):
-            return 0 <= c < NCH
-
-        for n in range(-2, NCH + 2):
-            if live(n - 2):
-                step_quantise_h(n - 2)
-            if live(n + 1):
-                step_compare(n + 1)
-                step_copy_x(n + 1)
-            if live(n - 1):
-                step_select(n - 1)
-                step_regroup(n - 1)
-            if live(n):
-                step_hidden(n)
-            if live(n + 1):
-                step_quantise_x(n + 1)
-            if live(n):
-                step_spread_masks(n)
-            if n == 0:
+        for c in range(NCH + 2):
+            if c >= 2:
+                back(c - 2)
+            if c < NCH:
+                front(c)
+            if c == 0:
                 prepare_wf()
-            if live(n + 2):
-                step_transpose(n + 2)
-                step_sum(n + 2)
-            if live(n - 2):
-                step_output(n - 2)
+            if 1 <= c <= NCH:
+                mid(c - 1)

@@ -143,13 +143,13 @@ def tile_dynamiclayer_t_kernel(tc, x, W1, b1, W2, b2, Wf, bf, out):
                 nc.scalar.activation(out=junk[:], in_=xc_sb[:, r * D:(r + 1) * D], func=ACT.Abs,
                                      accum_out=ssum[:, r:r + 1])
             mcol = work.tile([P, 4], BF16, tag="mcol")
-            nc.gpsimd.tensor_scalar(out=mcol[:], in0=ssum[:], scalar1=float(D), scalar2=None,
+            nc.vector.tensor_scalar(out=mcol[:], in0=ssum[:], scalar1=float(D), scalar2=None,
                                     op0=ALU.is_gt)
             nl = work.tile([P, 2 * P], BF16, tag="nl")
-            nc.gpsimd.tensor_scalar(
+            nc.scalar.activation(
                 out=nl[:].rearrange("p (r h c) -> p r h c", r=2, h=2),
-                in0=ssum[:].rearrange("p (h r) -> p r h", h=2).unsqueeze(3).to_broadcast([P, 2, 2, H]),
-                scalar1=float(D), scalar2=None, op0=ALU.is_le)
+                in_=mcol[:].rearrange("p (h r) -> p r h", h=2).unsqueeze(3).to_broadcast([P, 2, 2, H]),
+                func=ACT.Copy, scale=-1.0, bias=1.0)
             xg = work.tile([P, CH * 4], BF16, tag="xg", align_bytes=64)
             gv = xg[:].bitcast(F32).rearrange("p (r j u) -> p r j u", r=4, u=2)
             xv = xc_sb.bitcast(F32)
@@ -200,8 +200,10 @@ def tile_dynamiclayer_t_kernel(tc, x, W1, b1, W2, b2, Wf, bf, out):
             nc.vector.tensor_tensor(out=rv[0:H, :, 0:HC], in0=rv[0:H, :, 0:HC], in1=rv[0:H, :, CH:SL], op=ALU.max)
             nc.vector.tensor_tensor(out=rv[H:P, :, HC:CH], in0=rv[H:P, :, HC:CH], in1=rv[H:P, :, CH:SL], op=ALU.max)
             hg = work.tile([P, CH * 4], BF16, tag="hg", align_bytes=64)
-            nc.vector.tensor_copy(out=hg[:, 0:512 * 4].rearrange("p (c i t) -> p c t i", i=4, t=4),
-                                  in_=rv[:, :, 0:512].rearrange("p t (c i) -> p c t i", i=4))
+            nc.vector.tensor_copy(out=hg[:, 0:384 * 4].rearrange("p (c i t) -> p c t i", i=4, t=4),
+                                  in_=rv[:, :, 0:384].rearrange("p t (c i) -> p c t i", i=4))
+            nc.scalar.copy(out=hg[:, 384 * 4:CH * 4].rearrange("p (c i t) -> p c t i", i=4, t=4),
+                           in_=rv[:, :, 384:CH].rearrange("p t (c i) -> p c t i", i=4))
             hc = work.tile([P, CH], U32, tag="hc", align_bytes=64)
             hs = work.tile([P, CH], U8, tag="hs", align_bytes=64)
             nc.vector.quantize_mx(out=hc[:].bitcast(FP8X4), scales=hs[:], in_=hg[:])

@@ -143,13 +143,13 @@ def tile_dynamiclayer_t_kernel(tc, x, W1, b1, W2, b2, Wf, bf, out):
                 nc.scalar.activation(out=junk[:], in_=xc_sb[:, r * D:(r + 1) * D], func=ACT.Abs,
                                      accum_out=ssum[:, r:r + 1])
             mcol = work.tile([P, 4], BF16, tag="mcol")
-            nc.vector.tensor_scalar(out=mcol[:], in0=ssum[:], scalar1=float(D), scalar2=None,
+            nc.gpsimd.tensor_scalar(out=mcol[:], in0=ssum[:], scalar1=float(D), scalar2=None,
                                     op0=ALU.is_gt)
             nl = work.tile([P, 2 * P], BF16, tag="nl")
-            nc.scalar.activation(
+            nc.gpsimd.tensor_scalar(
                 out=nl[:].rearrange("p (r h c) -> p r h c", r=2, h=2),
-                in_=mcol[:].rearrange("p (h r) -> p r h", h=2).unsqueeze(3).to_broadcast([P, 2, 2, H]),
-                func=ACT.Copy, scale=-1.0, bias=1.0)
+                in0=ssum[:].rearrange("p (h r) -> p r h", h=2).unsqueeze(3).to_broadcast([P, 2, 2, H]),
+                scalar1=float(D), scalar2=None, op0=ALU.is_le)
             xg = work.tile([P, CH * 4], BF16, tag="xg", align_bytes=64)
             gv = xg[:].bitcast(F32).rearrange("p (r j u) -> p r j u", r=4, u=2)
             xv = xc_sb.bitcast(F32)
@@ -200,10 +200,10 @@ def tile_dynamiclayer_t_kernel(tc, x, W1, b1, W2, b2, Wf, bf, out):
             nc.vector.tensor_tensor(out=rv[0:H, :, 0:HC], in0=rv[0:H, :, 0:HC], in1=rv[0:H, :, CH:SL], op=ALU.max)
             nc.vector.tensor_tensor(out=rv[H:P, :, HC:CH], in0=rv[H:P, :, HC:CH], in1=rv[H:P, :, CH:SL], op=ALU.max)
             hg = work.tile([P, CH * 4], BF16, tag="hg", align_bytes=64)
-            nc.vector.tensor_copy(out=hg[:, 0:384 * 4].rearrange("p (c i t) -> p c t i", i=4, t=4),
-                                  in_=rv[:, :, 0:384].rearrange("p t (c i) -> p c t i", i=4))
-            nc.scalar.copy(out=hg[:, 384 * 4:CH * 4].rearrange("p (c i t) -> p c t i", i=4, t=4),
-                           in_=rv[:, :, 384:CH].rearrange("p t (c i) -> p c t i", i=4))
+            nc.vector.tensor_copy(out=hg[:, 0:256 * 4].rearrange("p (c i t) -> p c t i", i=4, t=4),
+                                  in_=rv[:, :, 0:256].rearrange("p t (c i) -> p c t i", i=4))
+            nc.scalar.copy(out=hg[:, 256 * 4:CH * 4].rearrange("p (c i t) -> p c t i", i=4, t=4),
+                           in_=rv[:, :, 256:CH].rearrange("p t (c i) -> p c t i", i=4))
             hc = work.tile([P, CH], U32, tag="hc", align_bytes=64)
             hs = work.tile([P, CH], U8, tag="hs", align_bytes=64)
             nc.vector.quantize_mx(out=hc[:].bitcast(FP8X4), scales=hs[:], in_=hg[:])

from contextlib import ExitStack

import concourse.mybir as mybir
from concourse.masks import make_identity

F32 = mybir.dt.float32
BF16 = mybir.dt.bfloat16
U32 = mybir.dt.uint32
U8 = mybir.dt.uint8
FP8X4 = mybir.dt.float8_e4m3fn_x4
ALU = mybir.AluOpType
ACT = mybir.ActivationFunctionType

P = 128
H = 64
B, D, U1, U2 = 8192, 512, 512, 256
FLOPS = 2 * B * D * (U1 + U2) + 2 * B * U1 * D
CH = 512
HC = CH // 2
SL = CH + HC
NCH = B // CH
SUP = 1024
NSUP = B // SUP


def tile_dynamiclayer_t_kernel(tc, x, W1, b1, W2, b2, Wf, bf, out):
    nc = tc.nc
    with ExitStack() as ctx:
        const = ctx.enter_context(tc.tile_pool(name="const", bufs=1))
        xpool = ctx.enter_context(tc.tile_pool(name="xpool", bufs=1))
        work = ctx.enter_context(tc.tile_pool(name="work", bufs=2))
        opool = ctx.enter_context(tc.tile_pool(name="opool", bufs=3))
        ps_x = ctx.enter_context(tc.psum_pool(name="ps_x", bufs=2))
        ps_z = ctx.enter_context(tc.psum_pool(name="ps_z", bufs=3))
        ps_y = ctx.enter_context(tc.psum_pool(name="ps_y", bufs=2))
        ps_m = ctx.enter_context(tc.psum_pool(name="ps_m", bufs=1))

        w1_sb = const.tile([P, 4 * D], BF16)
        w2_sb = const.tile([P, 4 * D], BF16)
        wf_sb = const.tile([P, 4 * 2 * U1], BF16)
        nc.vector.memset(w2_sb[H:P, :], 0.0)
        nc.sync.dma_start(out=w1_sb[:], in_=W1.rearrange("(m t) k -> m (t k)", t=4))
        nc.sync.dma_start(out=w2_sb[0:H, :], in_=W2.rearrange("(m t) k -> m (t k)", t=4))
        x_view = x.rearrange("(s p r) k -> s p (r k)", p=P, r=SUP // P)
        xs = []
        for s in range(NSUP):
            xt_sb = xpool.tile([P, (SUP // P) * D], BF16, name="x%d" % s)
            xs.append(xt_sb)
        nc.sync.dma_start(out=xs[0][:], in_=x_view[0])
        wf_dst = wf_sb[:].rearrange("p (a h u) -> p a h u", a=4, h=2)
        for h in range(2):
            nc.sync.dma_start(out=wf_dst[:, :, h, :], in_=Wf.rearrange("(a p) u -> p a u", p=P))
        for s in range(1, NSUP):
            nc.sync.dma_start(out=xs[s][:], in_=x_view[s])

        bb1 = const.tile([P, 4], BF16)
        bb1r = const.tile([P, 4], BF16)
        bb2 = const.tile([P, 4], BF16)
        b1v = b1.rearrange("(p t) -> p t", t=4)
        b2v = b2.rearrange("(p t) -> p t", t=4)
        with nc.allow_non_contiguous_dma(reason="four bias values to a partition"):
            nc.scalar.dma_start(out=bb1[:], in_=b1v)
            nc.scalar.dma_start(out=bb1r[0:H, :], in_=b1v[H:P, :])
            nc.scalar.dma_start(out=bb1r[H:P, :], in_=b1v[0:H, :])
            nc.scalar.dma_start(out=bb2[0:H, :], in_=b2v)
            nc.scalar.dma_start(out=bb2[H:P, :], in_=b2v)
        bfb = const.tile([P, D], BF16)
        nc.gpsimd.dma_start(out=bfb[:], in_=bf.partition_broadcast(P))

        ident_f = const.tile([P, P], F32)
        make_identity(nc, ident_f[:])
        ident_b = const.tile([P, P], BF16)
        make_identity(nc, ident_b[:])

        bc1 = const.tile([P, 4], F32)
        bc1r = const.tile([P, 4], F32)
        bc2 = const.tile([P, 4], F32)
        nc.vector.tensor_copy(out=bc1[:], in_=bb1[:])
        nc.vector.tensor_copy(out=bc1r[:], in_=bb1r[:])
        nc.vector.tensor_copy(out=bc2[:], in_=bb2[:])

        def bank_of_transposes(srcs, dsts, copy_engine):
            xt = ps_x.tile([P, 512], F32, tag="xt")
            for n in range(4):
                nc.tensor.transpose(xt[:, n * P:(n + 1) * P], srcs[n], ident_f[:])
            src = xt[:].rearrange("p (r u j) -> p r j u", r=2, u=2)
            for dst in dsts:
                if copy_engine == "s":
                    nc.scalar.copy(out=dst, in_=src)
                else:
                    nc.vector.tensor_copy(out=dst, in_=src)

        def halves(src_f32, tile_index):
            base = tile_index * 256
            return [src_f32[:, base:base + P], src_f32[:, base + P:base + 2 * P]]

        def stationary(w_sb, engine):
            g = const.tile([P, 4 * 2 * P * 4], BF16, align_bytes=64, name="g_" + engine)
            codes = const.tile([P, 4 * 2 * P], U32, align_bytes=64, name="c_" + engine)
            scales = const.tile([P, 4 * 2 * P], U8, align_bytes=64, name="s_" + engine)
            gv = g[:].bitcast(F32).rearrange("p (t d j u) -> p t d j u", t=4, d=2, u=2)
            wv = w_sb[:].bitcast(F32)
            for q in range(2):
                bank_of_transposes(halves(wv, 2 * q) + halves(wv, 2 * q + 1),
                                   [gv[:, 2 * q:2 * q + 2, 0], gv[:, 2 * q:2 * q + 2, 1]], engine)
            nc.vector.quantize_mx(out=codes[:].bitcast(FP8X4), scales=scales[:], in_=g[:])
            return codes, scales

        w1c, w1s = stationary(w1_sb, "v")
        w2c, w2s = stationary(w2_sb, "s")

        def slot(codes, scales, t, shifted):
            lo = t * 2 * P + (H if shifted else 0)
            return codes[:, lo:lo + P].bitcast(FP8X4), scales[:, lo:lo + P]

        wfq = []

        def prepare_wf():
            wv = wf_sb[:].bitcast(F32)
            for shifted in range(2):
                g = const.tile([P, D * 4], BF16, align_bytes=64, name="wfg%d" % shifted)
                codes = const.tile([P, D], U32, align_bytes=64, name="wfc%d" % shifted)
                scales = const.tile([P, D], U8, align_bytes=64, name="wfs%d" % shifted)
                gv = g[:].bitcast(F32).rearrange("p (a j u) -> p a j u", a=4, u=2)
                for q in range(2):
                    srcs = []
                    for a in (2 * q, 2 * q + 1):
                        for u in range(2):
                            lo = a * 512 + shifted * P + u
                            srcs.append(wv[:, lo:lo + 256:2])
                    bank_of_transposes(srcs, [gv[:, 2 * q:2 * q + 2]], "v")
                nc.vector.quantize_mx(out=codes[:].bitcast(FP8X4), scales=scales[:], in_=g[:])
                wfq.append((codes, scales))

        state = {}

        def front(c):
            s, h = c // 2, c % 2
            xc_sb = xs[s][:, h * 4 * D:(h + 1) * 4 * D]
            ssum = work.tile([P, 4], F32, tag="ssum")
            for r in range(4):
                junk = work.tile([P, D], BF16, tag="junk")
                nc.scalar.activation(out=junk[:], in_=xc_sb[:, r * D:(r + 1) * D], func=ACT.Abs,
                                     accum_out=ssum[:, r:r + 1])
            mcol = work.tile([P, 4], BF16, tag="mcol")
            nc.gpsimd.tensor_scalar(out=mcol[:], in0=ssum[:], scalar1=float(D), scalar2=None,
                                    op0=ALU.is_gt)
            nl = work.tile([P, 2 * P], BF16, tag="nl")
            nc.gpsimd.tensor_scalar(
                out=nl[:].rearrange("p (r h c) -> p r h c", r=2, h=2),
                in0=ssum[:].rearrange("p (h r) -> p r h", h=2).unsqueeze(3).to_broadcast([P, 2, 2, H]),
                scalar1=float(D), scalar2=None, op0=ALU.is_le)
            xg = work.tile([P, CH * 4], BF16, tag="xg", align_bytes=64)
            gv = xg[:].bitcast(F32).rearrange("p (r j u) -> p r j u", r=4, u=2)
            xv = xc_sb.bitcast(F32)
            for q in range(2):
                bank_of_transposes(halves(xv, 2 * q) + halves(xv, 2 * q + 1), [gv[:, 2 * q:2 * q + 2]], "s")
            xc = work.tile([P, CH], U32, tag="xc", align_bytes=64)
            xsc = work.tile([P, CH], U8, tag="xsc", align_bytes=64)
            nc.vector.quantize_mx(out=xc[:].bitcast(FP8X4), scales=xsc[:], in_=xg[:])
            state[("x", c)] = (xc, xsc, mcol, nl)

        def mid(c):
            xc, xsc, mcol, nl = state[("x", c)]
            mb = ps_m.tile([P, CH + HC], BF16, tag="mb")
            for r in range(4):
                nc.tensor.matmul(out=mb[:, r * P:(r + 1) * P], lhsT=mcol[:, r:r + 1].to_broadcast([P, P]),
                                 rhs=ident_b[:], start=True, stop=True)
            for r in range(2):
                nc.tensor.matmul(out=mb[:, CH + r * P:CH + (r + 1) * P], lhsT=nl[:, r * P:(r + 1) * P],
                                 rhs=ident_b[:], start=True, stop=True)
            half = [(xc[:, g * HC:(g + 1) * HC].bitcast(FP8X4), xsc[:, g * HC:(g + 1) * HC]) for g in range(2)]
            rr = work.tile([P, 4 * SL], BF16, tag="rr")
            for t in range(4):
                z = ps_z.tile([P, CH], F32, tag="z")
                for g in range(2):
                    wc, ws = slot(w1c, w1s, t, g == 1)
                    nc.tensor.matmul_mx(out=z[:, g * HC:(g + 1) * HC], lhsT=wc, lhsT_scale=ws,
                                        rhs=half[g][0], rhs_scale=half[g][1], start=True, stop=True)
                for g in range(2):
                    bias = bc1r if g == 1 else bc1
                    nc.scalar.activation(out=rr[:, t * SL + g * HC:t * SL + (g + 1) * HC],
                                         in_=z[:, g * HC:(g + 1) * HC], func=ACT.Relu,
                                         bias=bias[:, t:t + 1], scale=1.0)
            for q in range(2):
                z = ps_z.tile([P, CH], F32, tag="z")
                for tt in range(2):
                    t = 2 * q + tt
                    for g in range(2):
                        wc, ws = slot(w2c, w2s, t, g == 1)
                        nc.tensor.matmul_mx(out=z[:, tt * HC:(tt + 1) * HC], lhsT=wc, lhsT_scale=ws,
                                            rhs=half[g][0], rhs_scale=half[g][1],
                                            start=(g == 0), stop=(g == 1))
                for tt in range(2):
                    t = 2 * q + tt
                    nc.scalar.activation(out=rr[:, t * SL + CH:(t + 1) * SL], in_=z[:, tt * HC:(tt + 1) * HC],
                                         func=ACT.Relu, bias=bc2[:, t:t + 1], scale=1.0)
            rv = rr[:].rearrange("p (t i) -> p t i", t=4)
            nc.vector.tensor_tensor(out=rv, in0=rv, in1=mb[:].unsqueeze(1).to_broadcast([P, 4, SL]), op=ALU.mult)
            nc.vector.tensor_tensor(out=rv[0:H, :, 0:HC], in0=rv[0:H, :, 0:HC], in1=rv[0:H, :, CH:SL], op=ALU.max)
            nc.vector.tensor_tensor(out=rv[H:P, :, HC:CH], in0=rv[H:P, :, HC:CH], in1=rv[H:P, :, CH:SL], op=ALU.max)
            hg = work.tile([P, CH * 4], BF16, tag="hg", align_bytes=64)
            nc.vector.tensor_copy(out=hg[:, 0:256 * 4].rearrange("p (c i t) -> p c t i", i=4, t=4),
                                  in_=rv[:, :, 0:256].rearrange("p t (c i) -> p c t i", i=4))
            nc.scalar.copy(out=hg[:, 256 * 4:CH * 4].rearrange("p (c i t) -> p c t i", i=4, t=4),
                           in_=rv[:, :, 256:CH].rearrange("p t (c i) -> p c t i", i=4))
            hc = work.tile([P, CH], U32, tag="hc", align_bytes=64)
            hs = work.tile([P, CH], U8, tag="hs", align_bytes=64)
            nc.vector.quantize_mx(out=hc[:].bitcast(FP8X4), scales=hs[:], in_=hg[:])
            state[("h", c)] = (hc, hs)

        out_view = out.rearrange("(s p r) d -> s p (r d)", p=P, r=SUP // P)

        def back(c):
            s, h = c // 2, c % 2
            hc, hs = state[("h", c)]
            osb = opool.tile([P, 4 * D], F32, tag="osb")
            for r in range(4):
                wc, ws = wfq[r // 2]
                y = ps_y.tile([P, D], F32, tag="y")
                nc.tensor.matmul_mx(out=y[:], lhsT=hc[:, r * P:(r + 1) * P].bitcast(FP8X4),
                                    lhsT_scale=hs[:, r * P:(r + 1) * P],
                                    rhs=wc[:].bitcast(FP8X4), rhs_scale=ws[:], start=True, stop=True)
                nc.vector.tensor_tensor(out=osb[:, r * D:(r + 1) * D], in0=y[:], in1=bfb[:], op=ALU.add)
            pieces = 4 if c == NCH - 1 else 1
            w = 4 * D // pieces
            for e in range(pieces):
                nc.sync.dma_start(out=out_view[s][:, h * 4 * D + e * w:h * 4 * D + (e + 1) * w],
                                  in_=osb[:, e * w:(e + 1) * w])

        for c in range(NCH + 2):
            if c >= 2:
                back(c - 2)
            if c < NCH:
                front(c)
            if c == 0:
                prepare_wf()
            if 1 <= c <= NCH:
                mid(c - 1)
